import numpy as np
import ml_dtypes


def mxq(x, axis, fmt="e4m3"):
    dtype, down = {"e4m3": (ml_dtypes.float8_e4m3fn, 7), "e5m2": (ml_dtypes.float8_e5m2, 14)}[fmt]
    v = np.moveaxis(np.asarray(x, np.float32).astype(ml_dtypes.bfloat16).astype(np.float64), axis, -1)
    blocks = v.reshape(v.shape[:-1] + (-1, 32))
    amax = np.abs(blocks).max(-1, keepdims=True)
    byte = np.maximum(np.where(amax > 0, np.frexp(amax)[1] - 1 + 127, 0) - down, 1)
    scale = np.exp2(byte - 127.0)
    codes = (blocks / scale).astype(np.float32).astype(dtype).astype(np.float64)
    return np.moveaxis((codes * scale).reshape(v.shape), -1, axis)


WIDE = False


def mx_kscale(k):
    if not WIDE:
        return np.ones(k)
    levels = np.array([10, -10, 5, -5, 0])
    if k % 512:
        return np.exp2(np.random.permutation(np.resize(levels, k // 32))).repeat(32)
    a = np.empty((k // 512, 16))
    for p in range(k // 512):
        a[p, :8] = np.random.permutation(np.resize(levels, 8))
        for g in range(8):
            far = levels[np.abs(levels - a[p, g]) >= 10]
            a[p, g + 8] = far[np.random.randint(len(far))]
    return np.exp2(a.ravel()).repeat(32)


BF16 = ml_dtypes.bfloat16


def bf(x):
    return np.asarray(x, np.float32).astype(BF16)


def f64(x):
    return np.asarray(x).astype(np.float64)


B, S, E, H, DK = 2, 256, 2048, 16, 128
HD = H * DK


def rotate_half(u):
    shp = u.shape
    u = u.reshape(shp[:-1] + (shp[-1] // 2, 2))
    u1, u2 = u[..., 0], u[..., 1]
    return np.stack((-u2, u1), axis=-1).reshape(shp)


def setup_inputs():
    s = mx_kscale(E)
    theta = np.repeat(np.random.uniform(-np.pi, np.pi, (S, DK // 2)), 2, axis=-1)
    return {"x": bf(np.random.standard_normal((B, S, E)) * s),
            "wq": bf(np.random.standard_normal((HD, E)) / np.sqrt(E) / s[None, :]),
            "wk": bf(np.random.standard_normal((HD, E)) / np.sqrt(E) / s[None, :]),
            "cos_tab": bf(np.cos(theta)),
            "sin_tab": bf(np.sin(theta))}


def reference(x, wq, wk, cos_tab, sin_tab):
    xq = mxq(f64(x), 2, "e4m3")
    c, sn = f64(cos_tab), f64(sin_tab)

    def proj(w):
        y = xq @ mxq(f64(w), 1, "e4m3").T
        return y.reshape(B, S, H, DK).transpose(0, 2, 1, 3)

    def rot(u):
        return u * c + rotate_half(u) * sn

    return rot(proj(wq)), rot(proj(wk))

@@ -1,0 +1,167 @@
+from contextlib import ExitStack
+
+import concourse.mybir as mybir
+from concourse.masks import make_identity
+
+F32 = mybir.dt.float32
+BF16 = mybir.dt.bfloat16
+U32 = mybir.dt.uint32
+U8 = mybir.dt.uint8
+FP8X4 = mybir.dt.float8_e4m3fn_x4
+MULT = mybir.AluOpType.mult
+ADD = mybir.AluOpType.add
+
+P = 128
+B, S, E, H, DK = 2, 256, 2048, 16, 128
+PAIRS = DK // 2
+K_PASS = 4 * P
+PASSES = E // K_PASS
+SLAB = 2 * P
+SLAB_HEADS = SLAB // DK
+W_SLABS = H * DK // SLAB
+N_SLABS = B + 2 * W_SLABS
+
+RAW_BUFS = 8
+LEAD = 1
+
+FLOPS = 2 * B * S * E * 2 * H * DK
+
+
+def tile_multiheadattention_pa_kernel(tc, x, wq, wk, cos_tab, sin_tab, out_0, out_1):
+    nc = tc.nc
+
+    slab_rows = [x[b] for b in range(B)]
+    for w in (wq, wk):
+        slab_rows.extend(w[SLAB * i : SLAB * (i + 1), :] for i in range(W_SLABS))
+
+    with ExitStack() as ctx:
+        const = ctx.enter_context(tc.tile_pool(name="const", bufs=1))
+        raw_pool = ctx.enter_context(tc.tile_pool(name="raw", bufs=RAW_BUFS))
+        mx_pool = ctx.enter_context(tc.tile_pool(name="mx", bufs=LEAD + 2))
+        rot_pool = ctx.enter_context(tc.tile_pool(name="rot", bufs=4 * B))
+        t_psum = ctx.enter_context(tc.psum_pool(name="t_psum", bufs=4))
+        u_psum = ctx.enter_context(tc.psum_pool(name="u_psum", bufs=4))
+        ctx.enter_context(tc.manual_schedule())
+
+        raw = {}
+        grouped = {}
+        codes = {}
+        scales = {}
+        u_bank, prod = {}, {}
+
+        def load(n):
+            raw[n] = raw_pool.tile([P, 2, E], BF16, name="raw", tag="raw")
+            nc.sync.dma_start(out=raw[n][:], in_=slab_rows[n].rearrange("(p r) k -> p r k", r=2))
+
+        def transpose(n):
+            h = 1 if n < B else SLAB_HEADS
+            grouped[n] = mx_pool.tile(
+                [P, PASSES * SLAB * 4], BF16, name="grouped", tag="grouped", align_bytes=64
+            )
+            words = grouped[n][:].bitcast(F32).rearrange(
+                "p (g h r i u) -> p g h r i u", g=PASSES, h=h, r=2, u=2
+            )
+            for g0 in range(0, PASSES, 2):
+                for r in range(2):
+                    row_tile = raw[n][:, r, :].bitcast(F32)
+                    bank = t_psum.tile([P, 2, 2, P], F32, name="t_bank", tag="t_bank")
+                    for g in range(2):
+                        for u in range(2):
+                            first = 2 * P * (g0 + g)
+                            nc.tensor.transpose(
+                                bank[:, g, u, :], row_tile[:, first + u : first + 2 * P : 2], identity[:]
+                            )
+                    nc.scalar.copy(
+                        out=words[:, g0 : g0 + 2, :, r, :, :],
+                        in_=bank[:].rearrange("p g u (h i) -> p g h i u", h=h),
+                    )
+
+        def quantise(n, g0):
+            if g0 == 0 and n < B:
+                codes[n] = const.tile([P, PASSES, SLAB], U32, name="x_codes%d" % n, align_bytes=64)
+                scales[n] = const.tile([P, PASSES, SLAB], U8, name="x_scales%d" % n, align_bytes=64)
+            elif g0 == 0:
+                codes[n] = mx_pool.tile([P, PASSES, SLAB], U32, name="codes", tag="codes", align_bytes=64)
+                scales[n] = mx_pool.tile([P, PASSES, SLAB], U8, name="scales", tag="scales", align_bytes=64)
+            nc.vector.quantize_mx(
+                out=codes[n][:, g0 : g0 + 2, :].rearrange("p g c -> p (g c)").bitcast(FP8X4),
+                scales=scales[n][:, g0 : g0 + 2, :].rearrange("p g c -> p (g c)"),
+                in_=grouped[n][:, 4 * SLAB * g0 : 4 * SLAB * (g0 + 2)],
+            )
+
+        def multiply(s):
+            n = B + s
+            for b in range(B):
+                u_bank[b] = u_psum.tile([P, 2, SLAB], F32, name="u_bank", tag="u_bank")
+                for j in range(2):
+                    for g in range(PASSES):
+                        nc.tensor.matmul_mx(
+                            out=u_bank[b][:, j, :],
+                            lhsT=codes[b][:, g, P * j : P * (j + 1)].bitcast(FP8X4),
+                            lhsT_scale=scales[b][:, g, P * j : P * (j + 1)],
+                            rhs=codes[n][:, g, :].bitcast(FP8X4),
+                            rhs_scale=scales[n][:, g, :],
+                            start=(g == 0),
+                            stop=(g == PASSES - 1),
+                        )
+
+        def products(b):
+            shape = [P, 2 * SLAB_HEADS * 2, PAIRS, 2]
+            sums = u_bank[b][:].rearrange("p j (m i) -> p (j m) i", i=PAIRS)
+            prod[b] = rot_pool.tile(shape, F32, name="prod", tag="prod")
+            nc.vector.tensor_tensor(
+                out=prod[b][:], in0=sums.unsqueeze(3).to_broadcast(shape), in1=table, op=MULT
+            )
+
+        def add_and_store(s, b):
+            out = out_0 if s < W_SLABS else out_1
+            head = SLAB_HEADS * (s % W_SLABS)
+            parts = prod[b][:].rearrange("p (j h r) i t -> p j h r (i t)", j=2, r=2)
+            rotated = rot_pool.tile([P, SLAB_HEADS, 2, DK], F32, name="rotated", tag="rotated")
+            nc.gpsimd.tensor_tensor(
+                out=rotated[:].rearrange("p h j d -> p j h d"),
+                in0=parts[:, :, :, 0, :],
+                in1=parts[:, :, :, 1, :],
+                op=ADD,
+            )
+            nc.sync.dma_start(
+                out=out[b, head : head + SLAB_HEADS].rearrange("h (p j) d -> p h (j d)", j=2),
+                in_=rotated[:].rearrange("p h j d -> p h (j d)"),
+            )
+
+        for n in range(RAW_BUFS):
+            load(n)
+
+        identity = const.tile([P, P], F32, name="identity")
+        make_identity(nc, identity[:])
+
+        cos_sb = const.tile([P, 2, DK], BF16, name="cos_sb")
+        sin_sb = const.tile([P, 2, DK], BF16, name="sin_sb")
+        nc.scalar.dma_start(out=cos_sb[:], in_=cos_tab.rearrange("(p j) d -> p j d", j=2))
+        nc.scalar.dma_start(out=sin_sb[:], in_=sin_tab.rearrange("(p j) d -> p j d", j=2))
+        cos_it = cos_sb[:].rearrange("p j (i t) -> p j i t", t=2)
+        sin_it = sin_sb[:].rearrange("p j (i t) -> p j i t", t=2)
+        factors = const.tile([P, 2, SLAB_HEADS, 2, PAIRS, 2], F32, name="factors")
+        for h in range(SLAB_HEADS):
+            nc.vector.tensor_copy(out=factors[:, :, h, 0, :, 0], in_=cos_it[:, :, :, 0])
+            nc.vector.tensor_copy(out=factors[:, :, h, 0, :, 1], in_=sin_it[:, :, :, 1])
+            nc.vector.tensor_scalar_mul(out=factors[:, :, h, 1, :, 0], in0=sin_it[:, :, :, 0], scalar1=-1.0)
+            nc.vector.tensor_copy(out=factors[:, :, h, 1, :, 1], in_=cos_it[:, :, :, 1])
+        table = factors[:].rearrange("p j h r i t -> p (j h r) i t")
+
+        for s in range(-(B + LEAD), 2 * W_SLABS):
+            t = s + B + LEAD
+            if t < N_SLABS:
+                transpose(t)
+                if t + RAW_BUFS < N_SLABS:
+                    load(t + RAW_BUFS)
+                quantise(t, 0)
+            if s >= 0:
+                multiply(s)
+                products(0)
+            if t < N_SLABS:
+                quantise(t, 2)
+            if s >= 0:
+                products(1)
+                add_and_store(s, 0)
+                add_and_store(s, 1)

@@ -22,6 +22,8 @@ W_SLABS = H * DK // SLAB
 N_SLABS = B + 2 * W_SLABS
 
 RAW_BUFS = 8
+PERM_LEAD = 2
+FIRST_ORDERED = B + 2
 LEAD = 1
 
 FLOPS = 2 * B * S * E * 2 * H * DK
@@ -37,6 +39,7 @@ def tile_multiheadattention_pa_kernel(tc, x, wq, wk, cos_tab, sin_tab, out_0, ou
     with ExitStack() as ctx:
         const = ctx.enter_context(tc.tile_pool(name="const", bufs=1))
         raw_pool = ctx.enter_context(tc.tile_pool(name="raw", bufs=RAW_BUFS))
+        perm_pool = ctx.enter_context(tc.tile_pool(name="perm", bufs=PERM_LEAD + 1))
         mx_pool = ctx.enter_context(tc.tile_pool(name="mx", bufs=LEAD + 2))
         rot_pool = ctx.enter_context(tc.tile_pool(name="rot", bufs=4 * B))
         t_psum = ctx.enter_context(tc.psum_pool(name="t_psum", bufs=4))
@@ -44,6 +47,7 @@ def tile_multiheadattention_pa_kernel(tc, x, wq, wk, cos_tab, sin_tab, out_0, ou
         ctx.enter_context(tc.manual_schedule())
 
         raw = {}
+        ordered = {}
         grouped = {}
         codes = {}
         scales = {}
@@ -52,6 +56,13 @@ def tile_multiheadattention_pa_kernel(tc, x, wq, wk, cos_tab, sin_tab, out_0, ou
         def load(n):
             raw[n] = raw_pool.tile([P, 2, E], BF16, name="raw", tag="raw")
             nc.sync.dma_start(out=raw[n][:], in_=slab_rows[n].rearrange("(p r) k -> p r k", r=2))
+
+        def reorder(n):
+            ordered[n] = perm_pool.tile([P, PASSES, 2, P], F32, name="ordered", tag="ordered")
+            nc.scalar.copy(
+                out=ordered[n][:],
+                in_=raw[n][:, 0, :].bitcast(F32).rearrange("p (g w u) -> p g u w", g=PASSES, u=2),
+            )
 
         def transpose(n):
             h = 1 if n < B else SLAB_HEADS
@@ -68,9 +79,11 @@ def tile_multiheadattention_pa_kernel(tc, x, wq, wk, cos_tab, sin_tab, out_0, ou
                     for g in range(2):
                         for u in range(2):
                             first = 2 * P * (g0 + g)
-                            nc.tensor.transpose(
-                                bank[:, g, u, :], row_tile[:, first + u : first + 2 * P : 2], identity[:]
-                            )
+                            if n in ordered and r == 0:
+                                words_in = ordered[n][:, g0 + g, u, :]
+                            else:
+                                words_in = row_tile[:, first + u : first + 2 * P : 2]
+                            nc.tensor.transpose(bank[:, g, u, :], words_in, identity[:])
                     nc.scalar.copy(
                         out=words[:, g0 : g0 + 2, :, r, :, :],
                         in_=bank[:].rearrange("p g u (h i) -> p g h i u", h=h),
@@ -153,6 +166,8 @@ def tile_multiheadattention_pa_kernel(tc, x, wq, wk, cos_tab, sin_tab, out_0, ou
             t = s + B + LEAD
             if t < N_SLABS:
                 transpose(t)
+                if FIRST_ORDERED <= t + PERM_LEAD < N_SLABS:
+                    reorder(t + PERM_LEAD)
                 if t + RAW_BUFS < N_SLABS:
                     load(t + RAW_BUFS)
                 quantise(t, 0)

@@ -41,6 +41,7 @@ def tile_multiheadattention_pa_kernel(tc, x, wq, wk, cos_tab, sin_tab, out_0, ou
         raw_pool = ctx.enter_context(tc.tile_pool(name="raw", bufs=RAW_BUFS))
         perm_pool = ctx.enter_context(tc.tile_pool(name="perm", bufs=PERM_LEAD + 1))
         mx_pool = ctx.enter_context(tc.tile_pool(name="mx", bufs=LEAD + 2))
+        prod_pool = ctx.enter_context(tc.tile_pool(name="prod", bufs=4 * B * SLAB_HEADS))
         rot_pool = ctx.enter_context(tc.tile_pool(name="rot", bufs=4 * B))
         t_psum = ctx.enter_context(tc.psum_pool(name="t_psum", bufs=4))
         u_psum = ctx.enter_context(tc.psum_pool(name="u_psum", bufs=4))
@@ -51,7 +52,9 @@ def tile_multiheadattention_pa_kernel(tc, x, wq, wk, cos_tab, sin_tab, out_0, ou
         grouped = {}
         codes = {}
         scales = {}
-        u_bank, prod = {}, {}
+        u_bank = {}
+        prod = {}
+        rotated = {}
 
         def load(n):
             raw[n] = raw_pool.tile([P, 2, E], BF16, name="raw", tag="raw")
@@ -118,28 +121,28 @@ def tile_multiheadattention_pa_kernel(tc, x, wq, wk, cos_tab, sin_tab, out_0, ou
                             stop=(g == PASSES - 1),
                         )
 
-        def products(b):
-            shape = [P, 2 * SLAB_HEADS * 2, PAIRS, 2]
-            sums = u_bank[b][:].rearrange("p j (m i) -> p (j m) i", i=PAIRS)
-            prod[b] = rot_pool.tile(shape, F32, name="prod", tag="prod")
+        def products(s, b, h):
+            shape = [P, 2, 2 * PAIRS, 2]
+            sums = u_bank[b][:, :, DK * h : DK * (h + 1)]
+            prod[s, b, h] = prod_pool.tile(shape, F32, name="prod", tag="prod")
             nc.vector.tensor_tensor(
-                out=prod[b][:], in0=sums.unsqueeze(3).to_broadcast(shape), in1=table, op=MULT
+                out=prod[s, b, h][:], in0=sums.unsqueeze(3).to_broadcast(shape), in1=table, op=MULT
             )
 
-        def add_and_store(s, b):
+        def add(engine, s, b, h):
+            if h == 0:
+                rotated[s, b] = rot_pool.tile([P, SLAB_HEADS, 2, DK], F32, name="rotated", tag="rotated")
+            parts = prod[s, b, h][:].rearrange("p j (r i) t -> p j r (i t)", r=2)
+            engine.tensor_tensor(
+                out=rotated[s, b][:, h], in0=parts[:, :, 0, :], in1=parts[:, :, 1, :], op=ADD
+            )
+
+        def store(s, b):
             out = out_0 if s < W_SLABS else out_1
             head = SLAB_HEADS * (s % W_SLABS)
-            parts = prod[b][:].rearrange("p (j h r) i t -> p j h r (i t)", j=2, r=2)
-            rotated = rot_pool.tile([P, SLAB_HEADS, 2, DK], F32, name="rotated", tag="rotated")
-            nc.gpsimd.tensor_tensor(
-                out=rotated[:].rearrange("p h j d -> p j h d"),
-                in0=parts[:, :, :, 0, :],
-                in1=parts[:, :, :, 1, :],
-                op=ADD,
-            )
             nc.sync.dma_start(
                 out=out[b, head : head + SLAB_HEADS].rearrange("h (p j) d -> p h (j d)", j=2),
-                in_=rotated[:].rearrange("p h j d -> p h (j d)"),
+                in_=rotated[s, b][:].rearrange("p h j d -> p h (j d)"),
             )
 
         for n in range(RAW_BUFS):
@@ -154,13 +157,12 @@ def tile_multiheadattention_pa_kernel(tc, x, wq, wk, cos_tab, sin_tab, out_0, ou
         nc.scalar.dma_start(out=sin_sb[:], in_=sin_tab.rearrange("(p j) d -> p j d", j=2))
         cos_it = cos_sb[:].rearrange("p j (i t) -> p j i t", t=2)
         sin_it = sin_sb[:].rearrange("p j (i t) -> p j i t", t=2)
-        factors = const.tile([P, 2, SLAB_HEADS, 2, PAIRS, 2], F32, name="factors")
-        for h in range(SLAB_HEADS):
-            nc.vector.tensor_copy(out=factors[:, :, h, 0, :, 0], in_=cos_it[:, :, :, 0])
-            nc.vector.tensor_copy(out=factors[:, :, h, 0, :, 1], in_=sin_it[:, :, :, 1])
-            nc.vector.tensor_scalar_mul(out=factors[:, :, h, 1, :, 0], in0=sin_it[:, :, :, 0], scalar1=-1.0)
-            nc.vector.tensor_copy(out=factors[:, :, h, 1, :, 1], in_=cos_it[:, :, :, 1])
-        table = factors[:].rearrange("p j h r i t -> p (j h r) i t")
+        factors = const.tile([P, 2, 2, PAIRS, 2], F32, name="factors")
+        nc.vector.tensor_copy(out=factors[:, :, 0, :, 0], in_=cos_it[:, :, :, 0])
+        nc.vector.tensor_copy(out=factors[:, :, 0, :, 1], in_=sin_it[:, :, :, 1])
+        nc.vector.tensor_scalar_mul(out=factors[:, :, 1, :, 0], in0=sin_it[:, :, :, 0], scalar1=-1.0)
+        nc.vector.tensor_copy(out=factors[:, :, 1, :, 1], in_=cos_it[:, :, :, 1])
+        table = factors[:].rearrange("p j r i t -> p j (r i) t")
 
         for s in range(-(B + LEAD), 2 * W_SLABS):
             t = s + B + LEAD
@@ -171,12 +173,19 @@ def tile_multiheadattention_pa_kernel(tc, x, wq, wk, cos_tab, sin_tab, out_0, ou
                 if t + RAW_BUFS < N_SLABS:
                     load(t + RAW_BUFS)
                 quantise(t, 0)
-            if s >= 0:
-                multiply(s)
-                products(0)
+            if s >= 1:
+                add(nc.vector, s - 1, B - 1, SLAB_HEADS - 1)
+                store(s - 1, B - 1)
             if t < N_SLABS:
                 quantise(t, 2)
             if s >= 0:
-                products(1)
-                add_and_store(s, 0)
-                add_and_store(s, 1)
+                multiply(s)
+                for b in range(B):
+                    for h in range(SLAB_HEADS):
+                        products(s, b, h)
+                        if (b, h) != (B - 1, SLAB_HEADS - 1):
+                            add(nc.gpsimd, s, b, h)
+                    if b < B - 1:
+                        store(s, b)
+        add(nc.vector, 2 * W_SLABS - 1, B - 1, SLAB_HEADS - 1)
+        store(2 * W_SLABS - 1, B - 1)

@@ -19,11 +19,13 @@ PASSES = E // K_PASS
 SLAB = 2 * P
 SLAB_HEADS = SLAB // DK
 W_SLABS = H * DK // SLAB
+LAST = 2 * W_SLABS - 1
 N_SLABS = B + 2 * W_SLABS
 
 RAW_BUFS = 8
 PERM_LEAD = 2
-FIRST_ORDERED = B + 2
+UNORDERED = B + 3
+ODD_PASSES = 2
 LEAD = 1
 
 FLOPS = 2 * B * S * E * 2 * H * DK
@@ -41,7 +43,7 @@ def tile_multiheadattention_pa_kernel(tc, x, wq, wk, cos_tab, sin_tab, out_0, ou
         raw_pool = ctx.enter_context(tc.tile_pool(name="raw", bufs=RAW_BUFS))
         perm_pool = ctx.enter_context(tc.tile_pool(name="perm", bufs=PERM_LEAD + 1))
         mx_pool = ctx.enter_context(tc.tile_pool(name="mx", bufs=LEAD + 2))
-        prod_pool = ctx.enter_context(tc.tile_pool(name="prod", bufs=4 * B * SLAB_HEADS))
+        prod_pool = ctx.enter_context(tc.tile_pool(name="prod", bufs=4 * B))
         rot_pool = ctx.enter_context(tc.tile_pool(name="rot", bufs=4 * B))
         t_psum = ctx.enter_context(tc.psum_pool(name="t_psum", bufs=4))
         u_psum = ctx.enter_context(tc.psum_pool(name="u_psum", bufs=4))
@@ -58,14 +60,18 @@ def tile_multiheadattention_pa_kernel(tc, x, wq, wk, cos_tab, sin_tab, out_0, ou
 
         def load(n):
             raw[n] = raw_pool.tile([P, 2, E], BF16, name="raw", tag="raw")
-            nc.sync.dma_start(out=raw[n][:], in_=slab_rows[n].rearrange("(p r) k -> p r k", r=2))
+            rows = slab_rows[n].rearrange("(p r) k -> p r k", r=2)
+            halves = (slice(0, E // 2), slice(E // 2, E)) if n <= B + 1 else (slice(0, E),)
+            row_tiles = (slice(0, 1), slice(1, 2)) if n == 0 else (slice(0, 2),)
+            for k in halves:
+                for r in row_tiles:
+                    nc.sync.dma_start(out=raw[n][:, r, k], in_=rows[:, r, k])
 
         def reorder(n):
-            ordered[n] = perm_pool.tile([P, PASSES, 2, P], F32, name="ordered", tag="ordered")
-            nc.scalar.copy(
-                out=ordered[n][:],
-                in_=raw[n][:, 0, :].bitcast(F32).rearrange("p (g w u) -> p g u w", g=PASSES, u=2),
-            )
+            for r, passes in ((0, PASSES), (1, ODD_PASSES)):
+                ordered[n, r] = perm_pool.tile([P, passes, 2, P], F32, name="ordered", tag="ordered%d" % r)
+                words = raw[n][:, r, :].bitcast(F32).rearrange("p (g w u) -> p g u w", g=PASSES, u=2)
+                nc.scalar.copy(out=ordered[n, r][:], in_=words[:, :passes])
 
         def transpose(n):
             h = 1 if n < B else SLAB_HEADS
@@ -82,8 +88,8 @@ def tile_multiheadattention_pa_kernel(tc, x, wq, wk, cos_tab, sin_tab, out_0, ou
                     for g in range(2):
                         for u in range(2):
                             first = 2 * P * (g0 + g)
-                            if n in ordered and r == 0:
-                                words_in = ordered[n][:, g0 + g, u, :]
+                            if n >= UNORDERED and (r == 0 or g0 + g < ODD_PASSES):
+                                words_in = ordered[n, r][:, g0 + g, u, :]
                             else:
                                 words_in = row_tile[:, first + u : first + 2 * P : 2]
                             nc.tensor.transpose(bank[:, g, u, :], words_in, identity[:])
@@ -108,11 +114,13 @@ def tile_multiheadattention_pa_kernel(tc, x, wq, wk, cos_tab, sin_tab, out_0, ou
         def multiply(s):
             n = B + s
             for b in range(B):
-                u_bank[b] = u_psum.tile([P, 2, SLAB], F32, name="u_bank", tag="u_bank")
                 for j in range(2):
+                    if j == 0 or s == LAST:
+                        bank = u_psum.tile([P, 2, SLAB], F32, name="u_bank", tag="u_bank")
+                    u_bank[b, j] = bank
                     for g in range(PASSES):
                         nc.tensor.matmul_mx(
-                            out=u_bank[b][:, j, :],
+                            out=bank[:, j, :],
                             lhsT=codes[b][:, g, P * j : P * (j + 1)].bitcast(FP8X4),
                             lhsT_scale=scales[b][:, g, P * j : P * (j + 1)],
                             rhs=codes[n][:, g, :].bitcast(FP8X4),
@@ -121,20 +129,27 @@ def tile_multiheadattention_pa_kernel(tc, x, wq, wk, cos_tab, sin_tab, out_0, ou
                             stop=(g == PASSES - 1),
                         )
 
-        def products(s, b, h):
+        def quarters(tile, s, i):
+            return tile[:, :, i] if s == LAST else tile[:, i]
+
+        def products(s, b, i):
+            if i == 0:
+                prod[s, b] = prod_pool.tile([P, SLAB_HEADS, 2, 2 * PAIRS, 2], F32, name="prod", tag="prod")
+                rotated[s, b] = rot_pool.tile([P, SLAB_HEADS, 2, DK], F32, name="rotated", tag="rotated")
             shape = [P, 2, 2 * PAIRS, 2]
-            sums = u_bank[b][:, :, DK * h : DK * (h + 1)]
-            prod[s, b, h] = prod_pool.tile(shape, F32, name="prod", tag="prod")
+            bank = u_bank[b, i if s == LAST else 0]
+            sums = quarters(bank[:].rearrange("p j (h m) -> p h j m", h=SLAB_HEADS), s, i)
             nc.vector.tensor_tensor(
-                out=prod[s, b, h][:], in0=sums.unsqueeze(3).to_broadcast(shape), in1=table, op=MULT
+                out=quarters(prod[s, b], s, i),
+                in0=sums.unsqueeze(3).to_broadcast(shape),
+                in1=quarters(factors[:].rearrange("p h j r i t -> p h j (r i) t"), s, i),
+                op=MULT,
             )
 
-        def add(engine, s, b, h):
-            if h == 0:
-                rotated[s, b] = rot_pool.tile([P, SLAB_HEADS, 2, DK], F32, name="rotated", tag="rotated")
-            parts = prod[s, b, h][:].rearrange("p j (r i) t -> p j r (i t)", r=2)
+        def add(engine, s, b, i):
+            parts = quarters(prod[s, b], s, i).rearrange("p x (r i) t -> p x r (i t)", r=2)
             engine.tensor_tensor(
-                out=rotated[s, b][:, h], in0=parts[:, :, 0, :], in1=parts[:, :, 1, :], op=ADD
+                out=quarters(rotated[s, b], s, i), in0=parts[:, :, 0, :], in1=parts[:, :, 1, :], op=ADD
             )
 
         def store(s, b):
@@ -157,18 +172,18 @@ def tile_multiheadattention_pa_kernel(tc, x, wq, wk, cos_tab, sin_tab, out_0, ou
         nc.scalar.dma_start(out=sin_sb[:], in_=sin_tab.rearrange("(p j) d -> p j d", j=2))
         cos_it = cos_sb[:].rearrange("p j (i t) -> p j i t", t=2)
         sin_it = sin_sb[:].rearrange("p j (i t) -> p j i t", t=2)
-        factors = const.tile([P, 2, 2, PAIRS, 2], F32, name="factors")
-        nc.vector.tensor_copy(out=factors[:, :, 0, :, 0], in_=cos_it[:, :, :, 0])
-        nc.vector.tensor_copy(out=factors[:, :, 0, :, 1], in_=sin_it[:, :, :, 1])
-        nc.vector.tensor_scalar_mul(out=factors[:, :, 1, :, 0], in0=sin_it[:, :, :, 0], scalar1=-1.0)
-        nc.vector.tensor_copy(out=factors[:, :, 1, :, 1], in_=cos_it[:, :, :, 1])
-        table = factors[:].rearrange("p j r i t -> p j (r i) t")
+        factors = const.tile([P, SLAB_HEADS, 2, 2, PAIRS, 2], F32, name="factors")
+        for h in range(SLAB_HEADS):
+            nc.vector.tensor_copy(out=factors[:, h, :, 0, :, 0], in_=cos_it[:, :, :, 0])
+            nc.vector.tensor_copy(out=factors[:, h, :, 0, :, 1], in_=sin_it[:, :, :, 1])
+            nc.vector.tensor_scalar_mul(out=factors[:, h, :, 1, :, 0], in0=sin_it[:, :, :, 0], scalar1=-1.0)
+            nc.vector.tensor_copy(out=factors[:, h, :, 1, :, 1], in_=cos_it[:, :, :, 1])
 
         for s in range(-(B + LEAD), 2 * W_SLABS):
             t = s + B + LEAD
             if t < N_SLABS:
                 transpose(t)
-                if FIRST_ORDERED <= t + PERM_LEAD < N_SLABS:
+                if UNORDERED <= t + PERM_LEAD < N_SLABS:
                     reorder(t + PERM_LEAD)
                 if t + RAW_BUFS < N_SLABS:
                     load(t + RAW_BUFS)
@@ -181,11 +196,12 @@ def tile_multiheadattention_pa_kernel(tc, x, wq, wk, cos_tab, sin_tab, out_0, ou
             if s >= 0:
                 multiply(s)
                 for b in range(B):
-                    for h in range(SLAB_HEADS):
-                        products(s, b, h)
-                        if (b, h) != (B - 1, SLAB_HEADS - 1):
-                            add(nc.gpsimd, s, b, h)
-                    if b < B - 1:
+                    for i in range(2):
+                        products(s, b, i)
+                        if b == 0 or (i == 0 and s != LAST):
+                            add(nc.gpsimd, s, b, i)
+                    if b == 0:
                         store(s, b)
-        add(nc.vector, 2 * W_SLABS - 1, B - 1, SLAB_HEADS - 1)
-        store(2 * W_SLABS - 1, B - 1)
+        for i in range(2):
+            add(nc.vector, LAST, B - 1, i)
+        store(LAST, B - 1)

from contextlib import ExitStack

import concourse.mybir as mybir
from concourse.masks import make_identity

F32 = mybir.dt.float32
BF16 = mybir.dt.bfloat16
U32 = mybir.dt.uint32
U8 = mybir.dt.uint8
FP8X4 = mybir.dt.float8_e4m3fn_x4
MULT = mybir.AluOpType.mult
ADD = mybir.AluOpType.add

P = 128
B, S, E, H, DK = 2, 256, 2048, 16, 128
PAIRS = DK // 2
K_PASS = 4 * P
PASSES = E // K_PASS
SLAB = 2 * P
SLAB_HEADS = SLAB // DK
W_SLABS = H * DK // SLAB
LAST = 2 * W_SLABS - 1
N_SLABS = B + 2 * W_SLABS

RAW_BUFS = 8
PERM_LEAD = 2
UNORDERED = B + 3
ODD_PASSES = 2
LEAD = 1

FLOPS = 2 * B * S * E * 2 * H * DK


def tile_multiheadattention_pa_kernel(tc, x, wq, wk, cos_tab, sin_tab, out_0, out_1):
    nc = tc.nc

    slab_rows = [x[b] for b in range(B)]
    for w in (wq, wk):
        slab_rows.extend(w[SLAB * i : SLAB * (i + 1), :] for i in range(W_SLABS))

    with ExitStack() as ctx:
        const = ctx.enter_context(tc.tile_pool(name="const", bufs=1))
        raw_pool = ctx.enter_context(tc.tile_pool(name="raw", bufs=RAW_BUFS))
        perm_pool = ctx.enter_context(tc.tile_pool(name="perm", bufs=PERM_LEAD + 1))
        mx_pool = ctx.enter_context(tc.tile_pool(name="mx", bufs=LEAD + 2))
        prod_pool = ctx.enter_context(tc.tile_pool(name="prod", bufs=4 * B))
        rot_pool = ctx.enter_context(tc.tile_pool(name="rot", bufs=4 * B))
        t_psum = ctx.enter_context(tc.psum_pool(name="t_psum", bufs=4))
        u_psum = ctx.enter_context(tc.psum_pool(name="u_psum", bufs=4))
        ctx.enter_context(tc.manual_schedule())

        raw = {}
        ordered = {}
        grouped = {}
        codes = {}
        scales = {}
        u_bank = {}
        prod = {}
        rotated = {}

        def load(n):
            raw[n] = raw_pool.tile([P, 2, E], BF16, name="raw", tag="raw")
            rows = slab_rows[n].rearrange("(p r) k -> p r k", r=2)
            halves = (slice(0, E // 2), slice(E // 2, E)) if n <= B + 1 else (slice(0, E),)
            row_tiles = (slice(0, 1), slice(1, 2)) if n == 0 else (slice(0, 2),)
            for k in halves:
                for r in row_tiles:
                    nc.sync.dma_start(out=raw[n][:, r, k], in_=rows[:, r, k])

        def reorder(n):
            for r, passes in ((0, PASSES), (1, ODD_PASSES)):
                ordered[n, r] = perm_pool.tile([P, passes, 2, P], F32, name="ordered", tag="ordered%d" % r)
                words = raw[n][:, r, :].bitcast(F32).rearrange("p (g w u) -> p g u w", g=PASSES, u=2)
                nc.scalar.copy(out=ordered[n, r][:], in_=words[:, :passes])

        def transpose(n):
            h = 1 if n < B else SLAB_HEADS
            grouped[n] = mx_pool.tile(
                [P, PASSES * SLAB * 4], BF16, name="grouped", tag="grouped", align_bytes=64
            )
            words = grouped[n][:].bitcast(F32).rearrange(
                "p (g h r i u) -> p g h r i u", g=PASSES, h=h, r=2, u=2
            )
            for g0 in range(0, PASSES, 2):
                for r in range(2):
                    row_tile = raw[n][:, r, :].bitcast(F32)
                    bank = t_psum.tile([P, 2, 2, P], F32, name="t_bank", tag="t_bank")
                    for g in range(2):
                        for u in range(2):
                            first = 2 * P * (g0 + g)
                            if n >= UNORDERED and (r == 0 or g0 + g < ODD_PASSES):
                                words_in = ordered[n, r][:, g0 + g, u, :]
                            else:
                                words_in = row_tile[:, first + u : first + 2 * P : 2]
                            nc.tensor.transpose(bank[:, g, u, :], words_in, identity[:])
                    nc.scalar.copy(
                        out=words[:, g0 : g0 + 2, :, r, :, :],
                        in_=bank[:].rearrange("p g u (h i) -> p g h i u", h=h),
                    )

        def quantise(n, g0):
            if g0 == 0 and n < B:
                codes[n] = const.tile([P, PASSES, SLAB], U32, name="x_codes%d" % n, align_bytes=64)
                scales[n] = const.tile([P, PASSES, SLAB], U8, name="x_scales%d" % n, align_bytes=64)
            elif g0 == 0:
                codes[n] = mx_pool.tile([P, PASSES, SLAB], U32, name="codes", tag="codes", align_bytes=64)
                scales[n] = mx_pool.tile([P, PASSES, SLAB], U8, name="scales", tag="scales", align_bytes=64)
            nc.vector.quantize_mx(
                out=codes[n][:, g0 : g0 + 2, :].rearrange("p g c -> p (g c)").bitcast(FP8X4),
                scales=scales[n][:, g0 : g0 + 2, :].rearrange("p g c -> p (g c)"),
                in_=grouped[n][:, 4 * SLAB * g0 : 4 * SLAB * (g0 + 2)],
            )

        def multiply(s):
            n = B + s
            for b in range(B):
                for j in range(2):
                    if j == 0 or s == LAST:
                        bank = u_psum.tile([P, 2, SLAB], F32, name="u_bank", tag="u_bank")
                    u_bank[b, j] = bank
                    for g in range(PASSES):
                        nc.tensor.matmul_mx(
                            out=bank[:, j, :],
                            lhsT=codes[b][:, g, P * j : P * (j + 1)].bitcast(FP8X4),
                            lhsT_scale=scales[b][:, g, P * j : P * (j + 1)],
                            rhs=codes[n][:, g, :].bitcast(FP8X4),
                            rhs_scale=scales[n][:, g, :],
                            start=(g == 0),
                            stop=(g == PASSES - 1),
                        )

        def quarters(tile, s, i):
            return tile[:, :, i] if s == LAST else tile[:, i]

        def products(s, b, i):
            if i == 0:
                prod[s, b] = prod_pool.tile([P, SLAB_HEADS, 2, 2 * PAIRS, 2], F32, name="prod", tag="prod")
                rotated[s, b] = rot_pool.tile([P, SLAB_HEADS, 2, DK], F32, name="rotated", tag="rotated")
            shape = [P, 2, 2 * PAIRS, 2]
            bank = u_bank[b, i if s == LAST else 0]
            sums = quarters(bank[:].rearrange("p j (h m) -> p h j m", h=SLAB_HEADS), s, i)
            nc.vector.tensor_tensor(
                out=quarters(prod[s, b], s, i),
                in0=sums.unsqueeze(3).to_broadcast(shape),
                in1=quarters(factors[:].rearrange("p h j r i t -> p h j (r i) t"), s, i),
                op=MULT,
            )

        def add(engine, s, b, i):
            parts = quarters(prod[s, b], s, i).rearrange("p x (r i) t -> p x r (i t)", r=2)
            engine.tensor_tensor(
                out=quarters(rotated[s, b], s, i), in0=parts[:, :, 0, :], in1=parts[:, :, 1, :], op=ADD
            )

        def store(s, b):
            out = out_0 if s < W_SLABS else out_1
            head = SLAB_HEADS * (s % W_SLABS)
            nc.sync.dma_start(
                out=out[b, head : head + SLAB_HEADS].rearrange("h (p j) d -> p h (j d)", j=2),
                in_=rotated[s, b][:].rearrange("p h j d -> p h (j d)"),
            )

        for n in range(RAW_BUFS):
            load(n)

        identity = const.tile([P, P], F32, name="identity")
        make_identity(nc, identity[:])

        cos_sb = const.tile([P, 2, DK], BF16, name="cos_sb")
        sin_sb = const.tile([P, 2, DK], BF16, name="sin_sb")
        nc.scalar.dma_start(out=cos_sb[:], in_=cos_tab.rearrange("(p j) d -> p j d", j=2))
        nc.scalar.dma_start(out=sin_sb[:], in_=sin_tab.rearrange("(p j) d -> p j d", j=2))
        cos_it = cos_sb[:].rearrange("p j (i t) -> p j i t", t=2)
        sin_it = sin_sb[:].rearrange("p j (i t) -> p j i t", t=2)
        factors = const.tile([P, SLAB_HEADS, 2, 2, PAIRS, 2], F32, name="factors")
        for h in range(SLAB_HEADS):
            nc.vector.tensor_copy(out=factors[:, h, :, 0, :, 0], in_=cos_it[:, :, :, 0])
            nc.vector.tensor_copy(out=factors[:, h, :, 0, :, 1], in_=sin_it[:, :, :, 1])
            nc.vector.tensor_scalar_mul(out=factors[:, h, :, 1, :, 0], in0=sin_it[:, :, :, 0], scalar1=-1.0)
            nc.vector.tensor_copy(out=factors[:, h, :, 1, :, 1], in_=cos_it[:, :, :, 1])

        for s in range(-(B + LEAD), 2 * W_SLABS):
            t = s + B + LEAD
            if t < N_SLABS:
                transpose(t)
                if UNORDERED <= t + PERM_LEAD < N_SLABS:
                    reorder(t + PERM_LEAD)
                if t + RAW_BUFS < N_SLABS:
                    load(t + RAW_BUFS)
                quantise(t, 0)
            if s >= 1:
                add(nc.vector, s - 1, B - 1, SLAB_HEADS - 1)
                store(s - 1, B - 1)
            if t < N_SLABS:
                quantise(t, 2)
            if s >= 0:
                multiply(s)
                for b in range(B):
                    for i in range(2):
                        products(s, b, i)
                        if b == 0 or (i == 0 and s != LAST):
                            add(nc.gpsimd, s, b, i)
                    if b == 0:
                        store(s, b)
        for i in range(2):
            add(nc.vector, LAST, B - 1, i)
        store(LAST, B - 1)
